import numpy as np
import ml_dtypes


def mxq(x, axis, fmt="e4m3"):
    dtype, down = {"e4m3": (ml_dtypes.float8_e4m3fn, 7), "e5m2": (ml_dtypes.float8_e5m2, 14)}[fmt]
    v = np.moveaxis(np.asarray(x, np.float32).astype(ml_dtypes.bfloat16).astype(np.float64), axis, -1)
    blocks = v.reshape(v.shape[:-1] + (-1, 32))
    amax = np.abs(blocks).max(-1, keepdims=True)
    byte = np.maximum(np.where(amax > 0, np.frexp(amax)[1] - 1 + 127, 0) - down, 1)
    scale = np.exp2(byte - 127.0)
    codes = (blocks / scale).astype(np.float32).astype(dtype).astype(np.float64)
    return np.moveaxis((codes * scale).reshape(v.shape), -1, axis)


WIDE = False


def mx_kscale(k):
    if not WIDE:
        return np.ones(k)
    levels = np.array([10, -10, 5, -5, 0])
    a = np.random.permutation(np.resize(levels, k // 512 * 4)).reshape(k // 512, 4)
    idx = np.arange(k)
    return np.exp2(a[idx // 512, idx % 128 // 32])


BF16 = ml_dtypes.bfloat16


def bf(x):
    return np.asarray(x, np.float32).astype(BF16)


def f64(x):
    return np.asarray(x).astype(np.float64)


E2M1 = np.array([0.0, 0.5, 1.0, 1.5, 2.0, 3.0, 4.0, 6.0, -0.0, -0.5, -1.0, -1.5, -2.0, -3.0, -4.0, -6.0])


def pack_weight(w, fmt):
    k, n = w.shape
    w = f64(bf(w)).reshape(k // 32, 32, n)
    amax = np.abs(w).max(1)
    if fmt == "e4m3":
        byte = np.frexp(amax)[1] - 1 + 127 - 7
    else:
        mant, ex = np.frexp(amax / 6.0)
        byte = np.where(mant > 0.5, ex, ex - 1) + 127
    byte = np.clip(np.where(amax > 0, byte, 1), 1, 254)
    scaled = (w * np.exp2(127.0 - byte)[:, None, :]).reshape(k, n).astype(np.float32)
    by_word = np.ascontiguousarray(scaled.reshape(k // 512, 128, 4, n).transpose(0, 1, 3, 2))
    if fmt == "e4m3":
        words = by_word.astype(ml_dtypes.float8_e4m3fn).view(np.uint8)
    else:
        c = by_word.astype(ml_dtypes.float4_e2m1fn).view(np.uint8) & 0xF
        words = c[..., 0::2] | (c[..., 1::2] << 4)
    return np.ascontiguousarray(words), np.ascontiguousarray(byte.astype(np.uint8).reshape(k // 512, 16, n))


def unpack_weight(words, scales, fmt):
    g, p, n, _ = words.shape
    if fmt == "e4m3":
        vals = np.ascontiguousarray(words).view(ml_dtypes.float8_e4m3fn).astype(np.float64)
    else:
        nib = np.empty((g, p, n, 4), np.uint8)
        nib[..., 0::2] = words & 0xF
        nib[..., 1::2] = words >> 4
        vals = E2M1[nib]
    vals = vals * np.repeat(np.exp2(scales.astype(np.float64) - 127.0), 8, axis=1)[..., None]
    return vals.transpose(0, 1, 3, 2).reshape(g * 512, n)

def pack4(w):
    words, scales = pack_weight(w, "e2m1")
    return words.reshape(words.shape[0], 128, -1), scales


def unpack4(words, scales):
    return unpack_weight(words.reshape(words.shape[0], 128, -1, 2), scales, "e2m1")


B, I, H, P = 128, 16384, 512, 1024
CLOCKS = (0.5, 0.8, 0.95, 0.999)
TWO_PI = 2.0 * np.pi


def sigmoid(v):
    return 1.0 / (1.0 + np.exp(-v))


def setup_inputs():
    s = mx_kscale(I)
    x = bf(np.random.standard_normal((B, I)) * s)
    h_state = bf(np.random.standard_normal((B, H)))
    local_angle = bf(np.random.uniform(0.0, TWO_PI, (B, H)))
    persistence = bf(np.repeat(np.asarray(CLOCKS), H // len(CLOCKS)))
    ih_words, ih_scales = pack4(np.random.standard_normal((I, 3 * H)) * 0.7 / np.sqrt(I) / s[:, None])
    hh_words, hh_scales = pack4(np.random.standard_normal((H, 3 * H)) * 0.7 / np.sqrt(H))
    bias = bf(np.random.standard_normal(3 * H) * 0.3)
    return {
        "x": x,
        "h_state": h_state,
        "local_angle": local_angle,
        "persistence": persistence,
        "weight_ih_words": ih_words,
        "weight_ih_scales": ih_scales,
        "weight_hh_words": hh_words,
        "weight_hh_scales": hh_scales,
        "bias": bias,
    }


def reference(x, h_state, local_angle, persistence, weight_ih_words, weight_ih_scales, weight_hh_words, weight_hh_scales, bias):
    h = f64(h_state)
    gates = ((mxq(f64(x), 1, "e4m3") @ unpack4(weight_ih_words, weight_ih_scales))
             + (mxq(h, 1, "e4m3") @ unpack4(weight_hh_words, weight_hh_scales)) + f64(bias))
    r_gate, z_gate, n_gate = np.split(gates, 3, axis=-1)
    r = sigmoid(r_gate)
    z = sigmoid(z_gate)
    n = np.tanh(r * n_gate)
    phi_shift = z * TWO_PI
    raw_angle = f64(local_angle) * f64(persistence) + phi_shift
    h_blend = (1.0 - z) * h + z * n
    return (h_blend, raw_angle)

@@ -1,0 +1,231 @@
+from contextlib import ExitStack
+
+import math
+
+import concourse.mybir as mybir
+from concourse.masks import make_identity
+
+F32 = mybir.dt.float32
+BF16 = mybir.dt.bfloat16
+I32 = mybir.dt.int32
+U32 = mybir.dt.uint32
+U8 = mybir.dt.uint8
+FP8X4 = mybir.dt.float8_e4m3fn_x4
+FP4X4 = mybir.dt.float4_e2m1fn_x4
+ALU = mybir.AluOpType
+ACT = mybir.ActivationFunctionType
+
+P = 128
+PACK = 4
+K_PASS = P * PACK
+I = 16384
+H = 512
+GATES = 3
+N = GATES * H
+IH_PASSES = I // K_PASS
+HH_PASS = IH_PASSES
+PASSES = IH_PASSES + 1
+SCALE_ROWS = K_PASS // 32
+
+PAIRS = PACK // 2
+WORDS_PER_PASS = K_PASS // 2
+PASSES_PER_BANK = 2
+QUANT_PASSES = 4
+X_LOAD_PASSES = 8
+WORD_LOAD_PASSES = 2
+SCALE_GROUPS = 2
+GROUP_PASSES = IH_PASSES // SCALE_GROUPS
+SCALE_LOAD_PASSES = 8
+
+R_GATE = 0
+Z_GATE = 1
+N_GATE = 2
+
+FLOPS = 2 * P * (I + H) * N
+
+
+def tile_yarnixcellv4_pa_k_kernel(
+    tc,
+    x,
+    h_state,
+    local_angle,
+    persistence,
+    weight_ih_words,
+    weight_ih_scales,
+    weight_hh_words,
+    weight_hh_scales,
+    bias,
+    out_0,
+    out_1,
+):
+    nc = tc.nc
+    ih_words = weight_ih_words.bitcast(I32)
+    hh_words = weight_hh_words.bitcast(I32)
+    ih_scales = weight_ih_scales.bitcast(I32)
+    hh_scales = weight_hh_scales.bitcast(I32)
+
+    with ExitStack() as ctx:
+        ctx.enter_context(tc.manual_schedule())
+        keep = ctx.enter_context(tc.tile_pool(name="keep", bufs=1))
+        weights = ctx.enter_context(tc.tile_pool(name="weights", bufs=IH_PASSES // WORD_LOAD_PASSES))
+        sums = ctx.enter_context(tc.psum_pool(name="sums", bufs=1))
+        banks = ctx.enter_context(tc.psum_pool(name="banks", bufs=8 - GATES))
+
+        ident = keep.tile([P, P], F32)
+        make_identity(nc, ident[:])
+        warm_in = keep.tile([P, 1], F32)
+        warm_out = keep.tile([P, 1], F32)
+        nc.vector.memset(warm_in[:], 0.0)
+        nc.scalar.activation(out=warm_out[:], in_=warm_in[:], func=ACT.Sigmoid)
+        ones = keep.tile([P, P], BF16)
+        nc.vector.memset(ones[:], 1.0)
+
+        h_sb = keep.tile([P, H], BF16)
+        angle_sb = keep.tile([P, H], BF16)
+        x_codes = keep.tile([P, PASSES, P], U32, align_bytes=64)
+        x_scales = keep.tile([P, PASSES, P], U8, align_bytes=64)
+        w_scales = keep.tile([P, PASSES, N], U8, align_bytes=64)
+        w_scales_i32 = w_scales[:].bitcast(I32)
+        hh_tile = keep.tile([P, 1, 2 * N], U8, align_bytes=64)
+        bias_all = keep.tile([P, N], F32)
+        angle_term = keep.tile([P, H], F32)
+
+        def load_scale_rows(first_pass, scale_rows):
+            passes = scale_rows.shape[0]
+            for q in range(SCALE_ROWS // 2):
+                partition = 32 * (q // 4) + q % 4
+                nc.sync.dma_start(
+                    out=w_scales_i32[partition:P:64, first_pass : first_pass + passes, :],
+                    in_=scale_rows[:, q : SCALE_ROWS : SCALE_ROWS // 2, :].rearrange("g q n -> q g n"),
+                )
+
+        with ExitStack() as early:
+            x_pool = early.enter_context(tc.tile_pool(name="x_pool", bufs=IH_PASSES // X_LOAD_PASSES))
+            stage = early.enter_context(tc.tile_pool(name="stage", bufs=3))
+            rows = early.enter_context(tc.tile_pool(name="rows", bufs=1))
+
+            row = rows.tile([P, N + H], BF16)
+            nc.vector.memset(row[:].bitcast(I32), 0)
+            nc.vector.memset(w_scales_i32, 0)
+
+            nc.sync.dma_start(out=h_sb[:], in_=h_state)
+            x_tiles = []
+            for c in range(IH_PASSES // X_LOAD_PASSES):
+                x_tile = x_pool.tile([P, X_LOAD_PASSES * K_PASS], BF16)
+                nc.sync.dma_start(
+                    out=x_tile[:], in_=x[:, c * X_LOAD_PASSES * K_PASS : (c + 1) * X_LOAD_PASSES * K_PASS]
+                )
+                x_tiles.append(x_tile)
+            nc.sync.dma_start(out=row[0:1, 0:N], in_=bias.unsqueeze(0))
+            nc.sync.dma_start(out=row[0:1, N : N + H], in_=persistence.unsqueeze(0))
+            nc.sync.dma_start(out=angle_sb[:], in_=local_angle)
+
+            load_scale_rows(HH_PASS, hh_scales)
+            word_tiles = []
+            for group in range(SCALE_GROUPS):
+                first = group * GROUP_PASSES
+                for g in range(first, first + GROUP_PASSES, SCALE_LOAD_PASSES):
+                    load_scale_rows(g, ih_scales[g : g + SCALE_LOAD_PASSES])
+                if group == 0:
+                    nc.sync.dma_start(out=hh_tile[:].bitcast(I32), in_=hh_words.rearrange("g p n -> p g n"))
+                for g in range(first, first + GROUP_PASSES, WORD_LOAD_PASSES):
+                    word_tile = weights.tile([P, WORD_LOAD_PASSES, 2 * N], U8, align_bytes=64)
+                    nc.sync.dma_start(
+                        out=word_tile[:].bitcast(I32),
+                        in_=ih_words[g : g + WORD_LOAD_PASSES].rearrange("g p n -> p g n"),
+                    )
+                    word_tiles.append(word_tile)
+
+            def quantise_passes(batch_rows, first_pass, passes):
+                words = batch_rows.bitcast(F32)
+                grouped = stage.tile([P, passes, P, PACK], BF16, tag="grouped", align_bytes=64)
+                grouped_words = grouped[:].bitcast(F32)
+                for j0 in range(0, passes, PASSES_PER_BANK):
+                    in_bank = min(PASSES_PER_BANK, passes - j0)
+                    bank = banks.tile([P, in_bank, PAIRS, P], F32, tag="bank")
+                    for j in range(in_bank):
+                        first_word = (j0 + j) * WORDS_PER_PASS
+                        for u in range(PAIRS):
+                            nc.tensor.transpose(
+                                bank[:, j, u, :],
+                                words[:, first_word + u : first_word + WORDS_PER_PASS : PAIRS],
+                                ident[:],
+                            )
+                    nc.scalar.copy(
+                        out=grouped_words[:, j0 : j0 + in_bank, :, :],
+                        in_=bank[:].rearrange("p j u b -> p j b u"),
+                    )
+                nc.vector.quantize_mx(
+                    out=x_codes[:, first_pass : first_pass + passes, :].rearrange("p g b -> p (g b)").bitcast(FP8X4),
+                    scales=x_scales[:, first_pass : first_pass + passes, :].rearrange("p g b -> p (g b)"),
+                    in_=grouped[:].rearrange("p g b t -> p (g b t)"),
+                )
+
+            quantise_passes(h_sb[:], HH_PASS, 1)
+            for g in range(0, IH_PASSES, QUANT_PASSES):
+                x_tile = x_tiles[g // X_LOAD_PASSES]
+                first_column = (g % X_LOAD_PASSES) * K_PASS
+                quantise_passes(x_tile[:, first_column : first_column + QUANT_PASSES * K_PASS], g, QUANT_PASSES)
+
+            for c in range(GATES + 1):
+                spread = banks.tile([P, H], F32, tag="bank")
+                nc.tensor.matmul(out=spread[:], lhsT=ones[:], rhs=row[:, c * H : (c + 1) * H], start=True, stop=True)
+                if c < GATES:
+                    nc.scalar.copy(out=bias_all[:, c * H : (c + 1) * H], in_=spread[:])
+                else:
+                    nc.vector.tensor_tensor(out=angle_term[:], in0=spread[:], in1=angle_sb[:], op=ALU.mult)
+
+        sum_r = sums.tile([P, H], F32)
+        sum_z = sums.tile([P, H], F32)
+        sum_n = sums.tile([P, H], F32)
+        gate_order = ((Z_GATE, sum_z), (R_GATE, sum_r), (N_GATE, sum_n))
+
+        def multiply(first_pass, word_tile, start, stop):
+            passes = word_tile.shape[1]
+            for gate, gate_sum in gate_order:
+                for j in range(passes):
+                    g = first_pass + j
+                    nc.tensor.matmul_mx(
+                        out=gate_sum[:],
+                        lhsT=x_codes[:, g, :].bitcast(FP8X4),
+                        lhsT_scale=x_scales[:, g, :],
+                        rhs=word_tile[:, j, gate * 2 * H : (gate + 1) * 2 * H].bitcast(FP4X4),
+                        rhs_scale=w_scales[:, g, gate * H : (gate + 1) * H],
+                        start=start and j == 0,
+                        stop=stop and j == passes - 1,
+                    )
+
+        multiply(HH_PASS, hh_tile, True, False)
+        for c, word_tile in enumerate(word_tiles):
+            multiply(c * WORD_LOAD_PASSES, word_tile, False, c == len(word_tiles) - 1)
+
+        cell = ctx.enter_context(tc.tile_pool(name="cell", bufs=1))
+        z_gate = cell.tile([P, H], F32)
+        r_gate = cell.tile([P, H], F32)
+        n_gate = cell.tile([P, H], F32)
+        z = cell.tile([P, H], F32)
+        r = cell.tile([P, H], F32)
+        n_arg = cell.tile([P, H], F32)
+        n = cell.tile([P, H], F32)
+        raw_angle = cell.tile([P, H], F32)
+        minus_kept = cell.tile([P, H], F32)
+        z_n = cell.tile([P, H], F32)
+        h_blend = cell.tile([P, H], F32)
+
+        nc.vector.tensor_tensor(out=z_gate[:], in0=sum_z[:], in1=bias_all[:, Z_GATE * H : (Z_GATE + 1) * H], op=ALU.add)
+        nc.scalar.activation(out=z[:], in_=z_gate[:], func=ACT.Sigmoid)
+        nc.vector.tensor_tensor(out=r_gate[:], in0=sum_r[:], in1=bias_all[:, R_GATE * H : (R_GATE + 1) * H], op=ALU.add)
+        nc.scalar.activation(out=r[:], in_=r_gate[:], func=ACT.Sigmoid)
+        nc.vector.tensor_tensor(out=n_gate[:], in0=sum_n[:], in1=bias_all[:, N_GATE * H : (N_GATE + 1) * H], op=ALU.add)
+        nc.vector.tensor_tensor(out=n_arg[:], in0=r[:], in1=n_gate[:], op=ALU.mult)
+        nc.scalar.activation(out=n[:], in_=n_arg[:], func=ACT.Tanh)
+        nc.vector.scalar_tensor_tensor(
+            out=raw_angle[:], in0=z[:], scalar=2.0 * math.pi, in1=angle_term[:], op0=ALU.mult, op1=ALU.add
+        )
+        nc.sync.dma_start(out=out_1, in_=raw_angle[:])
+        nc.vector.scalar_tensor_tensor(
+            out=minus_kept[:], in0=z[:], scalar=1.0, in1=h_sb[:], op0=ALU.subtract, op1=ALU.mult
+        )
+        nc.vector.tensor_tensor(out=z_n[:], in0=z[:], in1=n[:], op=ALU.mult)
+        nc.vector.tensor_tensor(out=h_blend[:], in0=z_n[:], in1=minus_kept[:], op=ALU.subtract)
+        nc.sync.dma_start(out=out_0, in_=h_blend[:])

@@ -23,19 +23,17 @@ H = 512
 GATES = 3
 N = GATES * H
 IH_PASSES = I // K_PASS
-HH_PASS = IH_PASSES
-PASSES = IH_PASSES + 1
 SCALE_ROWS = K_PASS // 32
 
 PAIRS = PACK // 2
 WORDS_PER_PASS = K_PASS // 2
 PASSES_PER_BANK = 2
 QUANT_PASSES = 4
-X_LOAD_PASSES = 8
+PART_PASSES = 8
+PARTS = IH_PASSES // PART_PASSES
 WORD_LOAD_PASSES = 2
-SCALE_GROUPS = 2
-GROUP_PASSES = IH_PASSES // SCALE_GROUPS
-SCALE_LOAD_PASSES = 8
+WORD_LOADS = PART_PASSES // WORD_LOAD_PASSES
+RUN_PARTS = 2
 
 R_GATE = 0
 Z_GATE = 1
@@ -67,7 +65,8 @@ def tile_yarnixcellv4_pa_k_kernel(
     with ExitStack() as ctx:
         ctx.enter_context(tc.manual_schedule())
         keep = ctx.enter_context(tc.tile_pool(name="keep", bufs=1))
-        weights = ctx.enter_context(tc.tile_pool(name="weights", bufs=IH_PASSES // WORD_LOAD_PASSES))
+        per_part = ctx.enter_context(tc.tile_pool(name="per_part", bufs=PARTS))
+        weights = ctx.enter_context(tc.tile_pool(name="weights", bufs=PARTS * WORD_LOADS))
         sums = ctx.enter_context(tc.psum_pool(name="sums", bufs=1))
         banks = ctx.enter_context(tc.psum_pool(name="banks", bufs=8 - GATES))
 
@@ -82,53 +81,60 @@ def tile_yarnixcellv4_pa_k_kernel(
 
         h_sb = keep.tile([P, H], BF16)
         angle_sb = keep.tile([P, H], BF16)
-        x_codes = keep.tile([P, PASSES, P], U32, align_bytes=64)
-        x_scales = keep.tile([P, PASSES, P], U8, align_bytes=64)
-        w_scales = keep.tile([P, PASSES, N], U8, align_bytes=64)
-        w_scales_i32 = w_scales[:].bitcast(I32)
-        hh_tile = keep.tile([P, 1, 2 * N], U8, align_bytes=64)
         bias_all = keep.tile([P, N], F32)
         angle_term = keep.tile([P, H], F32)
+        h_codes = keep.tile([P, 1, P], U32, align_bytes=64)
+        h_scales = keep.tile([P, 1, P], U8, align_bytes=64)
+        hh_planes = keep.tile([P, 1, N], U8, align_bytes=64)
+        hh_tile = keep.tile([P, 1, 2 * N], U8, align_bytes=64)
+        x_codes = []
+        x_scales = []
+        w_planes = []
+        for part in range(PARTS):
+            x_codes.append(per_part.tile([P, PART_PASSES, P], U32, name="x_codes", align_bytes=64))
+            x_scales.append(per_part.tile([P, PART_PASSES, P], U8, name="x_scales", align_bytes=64))
+            w_planes.append(per_part.tile([P, PART_PASSES, N], U8, name="w_planes", align_bytes=64))
 
-        def load_scale_rows(first_pass, scale_rows):
-            passes = scale_rows.shape[0]
+        def load_scale_rows(planes, scale_rows):
             for q in range(SCALE_ROWS // 2):
                 partition = 32 * (q // 4) + q % 4
                 nc.sync.dma_start(
-                    out=w_scales_i32[partition:P:64, first_pass : first_pass + passes, :],
+                    out=planes[:].bitcast(I32)[partition:P:64, :, :],
                     in_=scale_rows[:, q : SCALE_ROWS : SCALE_ROWS // 2, :].rearrange("g q n -> q g n"),
                 )
 
         with ExitStack() as early:
-            x_pool = early.enter_context(tc.tile_pool(name="x_pool", bufs=IH_PASSES // X_LOAD_PASSES))
+            x_pool = early.enter_context(tc.tile_pool(name="x_pool", bufs=PARTS))
             stage = early.enter_context(tc.tile_pool(name="stage", bufs=3))
             rows = early.enter_context(tc.tile_pool(name="rows", bufs=1))
 
             row = rows.tile([P, N + H], BF16)
             nc.vector.memset(row[:].bitcast(I32), 0)
-            nc.vector.memset(w_scales_i32, 0)
+            nc.vector.memset(hh_planes[:].bitcast(I32), 0)
+            for part in range(PARTS):
+                nc.vector.memset(w_planes[part][:].bitcast(I32), 0)
 
             nc.sync.dma_start(out=h_sb[:], in_=h_state)
             x_tiles = []
-            for c in range(IH_PASSES // X_LOAD_PASSES):
-                x_tile = x_pool.tile([P, X_LOAD_PASSES * K_PASS], BF16)
+            for part in range(PARTS):
+                x_tile = x_pool.tile([P, PART_PASSES * K_PASS], BF16)
                 nc.sync.dma_start(
-                    out=x_tile[:], in_=x[:, c * X_LOAD_PASSES * K_PASS : (c + 1) * X_LOAD_PASSES * K_PASS]
+                    out=x_tile[:], in_=x[:, part * PART_PASSES * K_PASS : (part + 1) * PART_PASSES * K_PASS]
                 )
                 x_tiles.append(x_tile)
             nc.sync.dma_start(out=row[0:1, 0:N], in_=bias.unsqueeze(0))
             nc.sync.dma_start(out=row[0:1, N : N + H], in_=persistence.unsqueeze(0))
             nc.sync.dma_start(out=angle_sb[:], in_=local_angle)
 
-            load_scale_rows(HH_PASS, hh_scales)
+            load_scale_rows(hh_planes, hh_scales)
             word_tiles = []
-            for group in range(SCALE_GROUPS):
-                first = group * GROUP_PASSES
-                for g in range(first, first + GROUP_PASSES, SCALE_LOAD_PASSES):
-                    load_scale_rows(g, ih_scales[g : g + SCALE_LOAD_PASSES])
-                if group == 0:
+            for first_part in range(0, PARTS, RUN_PARTS):
+                run = range(first_part, first_part + RUN_PARTS)
+                for part in run:
+                    load_scale_rows(w_planes[part], ih_scales[part * PART_PASSES : (part + 1) * PART_PASSES])
+                if first_part == 0:
                     nc.sync.dma_start(out=hh_tile[:].bitcast(I32), in_=hh_words.rearrange("g p n -> p g n"))
-                for g in range(first, first + GROUP_PASSES, WORD_LOAD_PASSES):
+                for g in range(run[0] * PART_PASSES, (run[-1] + 1) * PART_PASSES, WORD_LOAD_PASSES):
                     word_tile = weights.tile([P, WORD_LOAD_PASSES, 2 * N], U8, align_bytes=64)
                     nc.sync.dma_start(
                         out=word_tile[:].bitcast(I32),
@@ -136,7 +142,8 @@ def tile_yarnixcellv4_pa_k_kernel(
                     )
                     word_tiles.append(word_tile)
 
-            def quantise_passes(batch_rows, first_pass, passes):
+            def quantise_passes(batch_rows, codes, scales):
+                passes = codes.shape[1]
                 words = batch_rows.bitcast(F32)
                 grouped = stage.tile([P, passes, P, PACK], BF16, tag="grouped", align_bytes=64)
                 grouped_words = grouped[:].bitcast(F32)
@@ -156,16 +163,19 @@ def tile_yarnixcellv4_pa_k_kernel(
                         in_=bank[:].rearrange("p j u b -> p j b u"),
                     )
                 nc.vector.quantize_mx(
-                    out=x_codes[:, first_pass : first_pass + passes, :].rearrange("p g b -> p (g b)").bitcast(FP8X4),
-                    scales=x_scales[:, first_pass : first_pass + passes, :].rearrange("p g b -> p (g b)"),
+                    out=codes.rearrange("p g b -> p (g b)").bitcast(FP8X4),
+                    scales=scales.rearrange("p g b -> p (g b)"),
                     in_=grouped[:].rearrange("p g b t -> p (g b t)"),
                 )
 
-            quantise_passes(h_sb[:], HH_PASS, 1)
-            for g in range(0, IH_PASSES, QUANT_PASSES):
-                x_tile = x_tiles[g // X_LOAD_PASSES]
-                first_column = (g % X_LOAD_PASSES) * K_PASS
-                quantise_passes(x_tile[:, first_column : first_column + QUANT_PASSES * K_PASS], g, QUANT_PASSES)
+            quantise_passes(h_sb[:], h_codes[:], h_scales[:])
+            for part in range(PARTS):
+                for j in range(0, PART_PASSES, QUANT_PASSES):
+                    quantise_passes(
+                        x_tiles[part][:, j * K_PASS : (j + QUANT_PASSES) * K_PASS],
+                        x_codes[part][:, j : j + QUANT_PASSES, :],
+                        x_scales[part][:, j : j + QUANT_PASSES, :],
+                    )
 
             for c in range(GATES + 1):
                 spread = banks.tile([P, H], F32, tag="bank")
@@ -180,24 +190,32 @@ def tile_yarnixcellv4_pa_k_kernel(
         sum_n = sums.tile([P, H], F32)
         gate_order = ((Z_GATE, sum_z), (R_GATE, sum_r), (N_GATE, sum_n))
 
-        def multiply(first_pass, word_tile, start, stop):
+        def multiply(codes, scales, planes, word_tile, start, stop):
             passes = word_tile.shape[1]
             for gate, gate_sum in gate_order:
                 for j in range(passes):
-                    g = first_pass + j
                     nc.tensor.matmul_mx(
                         out=gate_sum[:],
-                        lhsT=x_codes[:, g, :].bitcast(FP8X4),
-                        lhsT_scale=x_scales[:, g, :],
+                        lhsT=codes[:, j, :].bitcast(FP8X4),
+                        lhsT_scale=scales[:, j, :],
                         rhs=word_tile[:, j, gate * 2 * H : (gate + 1) * 2 * H].bitcast(FP4X4),
-                        rhs_scale=w_scales[:, g, gate * H : (gate + 1) * H],
+                        rhs_scale=planes[:, j, gate * H : (gate + 1) * H],
                         start=start and j == 0,
                         stop=stop and j == passes - 1,
                     )
 
-        multiply(HH_PASS, hh_tile, True, False)
+        multiply(h_codes, h_scales, hh_planes, hh_tile, True, False)
         for c, word_tile in enumerate(word_tiles):
-            multiply(c * WORD_LOAD_PASSES, word_tile, False, c == len(word_tiles) - 1)
+            part = c // WORD_LOADS
+            j = (c % WORD_LOADS) * WORD_LOAD_PASSES
+            multiply(
+                x_codes[part][:, j : j + WORD_LOAD_PASSES, :],
+                x_scales[part][:, j : j + WORD_LOAD_PASSES, :],
+                w_planes[part][:, j : j + WORD_LOAD_PASSES, :],
+                word_tile,
+                False,
+                c == len(word_tiles) - 1,
+            )
 
         cell = ctx.enter_context(tc.tile_pool(name="cell", bufs=1))
         z_gate = cell.tile([P, H], F32)

@@ -95,12 +95,13 @@ def tile_yarnixcellv4_pa_k_kernel(
             x_scales.append(per_part.tile([P, PART_PASSES, P], U8, name="x_scales", align_bytes=64))
             w_planes.append(per_part.tile([P, PART_PASSES, N], U8, name="w_planes", align_bytes=64))
 
-        def load_scale_rows(planes, scale_rows):
-            for q in range(SCALE_ROWS // 2):
+        def load_scale_rows(planes, scale_rows, apart):
+            rows_apart = apart // 8
+            for q in range(rows_apart):
                 partition = 32 * (q // 4) + q % 4
                 nc.sync.dma_start(
-                    out=planes[:].bitcast(I32)[partition:P:64, :, :],
-                    in_=scale_rows[:, q : SCALE_ROWS : SCALE_ROWS // 2, :].rearrange("g q n -> q g n"),
+                    out=planes[:].bitcast(I32)[partition:P:apart, :, :],
+                    in_=scale_rows[:, q:SCALE_ROWS:rows_apart, :].rearrange("g q n -> q g n"),
                 )
 
         with ExitStack() as early:
@@ -114,7 +115,11 @@ def tile_yarnixcellv4_pa_k_kernel(
             for part in range(PARTS):
                 nc.vector.memset(w_planes[part][:].bitcast(I32), 0)
 
-            nc.sync.dma_start(out=h_sb[:], in_=h_state)
+            nc.gpsimd.dma_start(out=h_sb[:], in_=h_state)
+            nc.gpsimd.dma_start(out=row[0:1, 0:N], in_=bias.unsqueeze(0))
+            nc.gpsimd.dma_start(out=row[0:1, N : N + H], in_=persistence.unsqueeze(0))
+            nc.gpsimd.dma_start(out=angle_sb[:], in_=local_angle)
+
             x_tiles = []
             for part in range(PARTS):
                 x_tile = x_pool.tile([P, PART_PASSES * K_PASS], BF16)
@@ -122,16 +127,14 @@ def tile_yarnixcellv4_pa_k_kernel(
                     out=x_tile[:], in_=x[:, part * PART_PASSES * K_PASS : (part + 1) * PART_PASSES * K_PASS]
                 )
                 x_tiles.append(x_tile)
-            nc.sync.dma_start(out=row[0:1, 0:N], in_=bias.unsqueeze(0))
-            nc.sync.dma_start(out=row[0:1, N : N + H], in_=persistence.unsqueeze(0))
-            nc.sync.dma_start(out=angle_sb[:], in_=local_angle)
+                if part == PARTS // 2 - 1:
+                    load_scale_rows(hh_planes, hh_scales, 32)
 
-            load_scale_rows(hh_planes, hh_scales)
             word_tiles = []
             for first_part in range(0, PARTS, RUN_PARTS):
                 run = range(first_part, first_part + RUN_PARTS)
                 for part in run:
-                    load_scale_rows(w_planes[part], ih_scales[part * PART_PASSES : (part + 1) * PART_PASSES])
+                    load_scale_rows(w_planes[part], ih_scales[part * PART_PASSES : (part + 1) * PART_PASSES], 64)
                 if first_part == 0:
                     nc.sync.dma_start(out=hh_tile[:].bitcast(I32), in_=hh_words.rearrange("g p n -> p g n"))
                 for g in range(run[0] * PART_PASSES, (run[-1] + 1) * PART_PASSES, WORD_LOAD_PASSES):
@@ -168,7 +171,6 @@ def tile_yarnixcellv4_pa_k_kernel(
                     in_=grouped[:].rearrange("p g b t -> p (g b t)"),
                 )
 
-            quantise_passes(h_sb[:], h_codes[:], h_scales[:])
             for part in range(PARTS):
                 for j in range(0, PART_PASSES, QUANT_PASSES):
                     quantise_passes(
@@ -176,6 +178,7 @@ def tile_yarnixcellv4_pa_k_kernel(
                         x_codes[part][:, j : j + QUANT_PASSES, :],
                         x_scales[part][:, j : j + QUANT_PASSES, :],
                     )
+            quantise_passes(h_sb[:], h_codes[:], h_scales[:])
 
             for c in range(GATES + 1):
                 spread = banks.tile([P, H], F32, tag="bank")

@@ -34,6 +34,7 @@ PARTS = IH_PASSES // PART_PASSES
 WORD_LOAD_PASSES = 2
 WORD_LOADS = PART_PASSES // WORD_LOAD_PASSES
 RUN_PARTS = 2
+SCALE_LOAD_PASSES = 4
 
 R_GATE = 0
 Z_GATE = 1
@@ -100,7 +101,7 @@ def tile_yarnixcellv4_pa_k_kernel(
             for q in range(rows_apart):
                 partition = 32 * (q // 4) + q % 4
                 nc.sync.dma_start(
-                    out=planes[:].bitcast(I32)[partition:P:apart, :, :],
+                    out=planes.bitcast(I32)[partition:P:apart, :, :],
                     in_=scale_rows[:, q:SCALE_ROWS:rows_apart, :].rearrange("g q n -> q g n"),
                 )
 
@@ -128,13 +129,17 @@ def tile_yarnixcellv4_pa_k_kernel(
                 )
                 x_tiles.append(x_tile)
                 if part == PARTS // 2 - 1:
-                    load_scale_rows(hh_planes, hh_scales, 32)
+                    load_scale_rows(hh_planes[:], hh_scales, 32)
 
             word_tiles = []
             for first_part in range(0, PARTS, RUN_PARTS):
                 run = range(first_part, first_part + RUN_PARTS)
                 for part in run:
-                    load_scale_rows(w_planes[part], ih_scales[part * PART_PASSES : (part + 1) * PART_PASSES], 64)
+                    for j in range(0, PART_PASSES, SCALE_LOAD_PASSES):
+                        g = part * PART_PASSES + j
+                        load_scale_rows(
+                            w_planes[part][:, j : j + SCALE_LOAD_PASSES, :], ih_scales[g : g + SCALE_LOAD_PASSES], 64
+                        )
                 if first_part == 0:
                     nc.sync.dma_start(out=hh_tile[:].bitcast(I32), in_=hh_words.rearrange("g p n -> p g n"))
                 for g in range(run[0] * PART_PASSES, (run[-1] + 1) * PART_PASSES, WORD_LOAD_PASSES):

@@ -34,7 +34,7 @@ PARTS = IH_PASSES // PART_PASSES
 WORD_LOAD_PASSES = 2
 WORD_LOADS = PART_PASSES // WORD_LOAD_PASSES
 RUN_PARTS = 2
-SCALE_LOAD_PASSES = 4
+SCALE_LOAD_PASSES = 2
 
 R_GATE = 0
 Z_GATE = 1

@@ -31,10 +31,10 @@ PASSES_PER_BANK = 2
 QUANT_PASSES = 4
 PART_PASSES = 8
 PARTS = IH_PASSES // PART_PASSES
-WORD_LOAD_PASSES = 2
+WORD_LOAD_PASSES = 1
 WORD_LOADS = PART_PASSES // WORD_LOAD_PASSES
 RUN_PARTS = 2
-SCALE_LOAD_PASSES = 2
+SCALE_LOAD_PASSES = 4
 
 R_GATE = 0
 Z_GATE = 1

@@ -34,7 +34,7 @@ PARTS = IH_PASSES // PART_PASSES
 WORD_LOAD_PASSES = 1
 WORD_LOADS = PART_PASSES // WORD_LOAD_PASSES
 RUN_PARTS = 2
-SCALE_LOAD_PASSES = 4
+RUN_PASSES = RUN_PARTS * PART_PASSES
 
 R_GATE = 0
 Z_GATE = 1
@@ -67,6 +67,7 @@ def tile_yarnixcellv4_pa_k_kernel(
         ctx.enter_context(tc.manual_schedule())
         keep = ctx.enter_context(tc.tile_pool(name="keep", bufs=1))
         per_part = ctx.enter_context(tc.tile_pool(name="per_part", bufs=PARTS))
+        per_run = ctx.enter_context(tc.tile_pool(name="per_run", bufs=PARTS // RUN_PARTS))
         weights = ctx.enter_context(tc.tile_pool(name="weights", bufs=PARTS * WORD_LOADS))
         sums = ctx.enter_context(tc.psum_pool(name="sums", bufs=1))
         banks = ctx.enter_context(tc.psum_pool(name="banks", bufs=8 - GATES))
@@ -94,7 +95,15 @@ def tile_yarnixcellv4_pa_k_kernel(
         for part in range(PARTS):
             x_codes.append(per_part.tile([P, PART_PASSES, P], U32, name="x_codes", align_bytes=64))
             x_scales.append(per_part.tile([P, PART_PASSES, P], U8, name="x_scales", align_bytes=64))
-            w_planes.append(per_part.tile([P, PART_PASSES, N], U8, name="w_planes", align_bytes=64))
+        for run in range(IH_PASSES // RUN_PASSES):
+            w_planes.append(per_run.tile([P, RUN_PASSES, N], U8, name="w_planes", align_bytes=64))
+
+        def load_scale_row(planes, scale_rows, q):
+            partition = 32 * (q // 4) + q % 4
+            nc.sync.dma_start(
+                out=planes.bitcast(I32)[partition : partition + 1, :, :],
+                in_=scale_rows[:, q : q + 1, :].rearrange("g q n -> q g n"),
+            )
 
         def load_scale_rows(planes, scale_rows, apart):
             rows_apart = apart // 8
@@ -113,8 +122,8 @@ def tile_yarnixcellv4_pa_k_kernel(
             row = rows.tile([P, N + H], BF16)
             nc.vector.memset(row[:].bitcast(I32), 0)
             nc.vector.memset(hh_planes[:].bitcast(I32), 0)
-            for part in range(PARTS):
-                nc.vector.memset(w_planes[part][:].bitcast(I32), 0)
+            for planes in w_planes:
+                nc.vector.memset(planes[:].bitcast(I32), 0)
 
             nc.gpsimd.dma_start(out=h_sb[:], in_=h_state)
             nc.gpsimd.dma_start(out=row[0:1, 0:N], in_=bias.unsqueeze(0))
@@ -134,12 +143,10 @@ def tile_yarnixcellv4_pa_k_kernel(
             word_tiles = []
             for first_part in range(0, PARTS, RUN_PARTS):
                 run = range(first_part, first_part + RUN_PARTS)
-                for part in run:
-                    for j in range(0, PART_PASSES, SCALE_LOAD_PASSES):
-                        g = part * PART_PASSES + j
-                        load_scale_rows(
-                            w_planes[part][:, j : j + SCALE_LOAD_PASSES, :], ih_scales[g : g + SCALE_LOAD_PASSES], 64
-                        )
+                run_scales = ih_scales[run[0] * PART_PASSES : run[0] * PART_PASSES + RUN_PASSES]
+                for q in range(SCALE_ROWS // 2):
+                    load_scale_row(w_planes[first_part // RUN_PARTS][:], run_scales, q)
+                    load_scale_row(w_planes[first_part // RUN_PARTS][:], run_scales, q + SCALE_ROWS // 2)
                 if first_part == 0:
                     nc.sync.dma_start(out=hh_tile[:].bitcast(I32), in_=hh_words.rearrange("g p n -> p g n"))
                 for g in range(run[0] * PART_PASSES, (run[-1] + 1) * PART_PASSES, WORD_LOAD_PASSES):
@@ -219,7 +226,7 @@ def tile_yarnixcellv4_pa_k_kernel(
             multiply(
                 x_codes[part][:, j : j + WORD_LOAD_PASSES, :],
                 x_scales[part][:, j : j + WORD_LOAD_PASSES, :],
-                w_planes[part][:, j : j + WORD_LOAD_PASSES, :],
+                w_planes[c // RUN_PASSES][:, c % RUN_PASSES : c % RUN_PASSES + WORD_LOAD_PASSES, :],
                 word_tile,
                 False,
                 c == len(word_tiles) - 1,

@@ -36,6 +36,8 @@ WORD_LOADS = PART_PASSES // WORD_LOAD_PASSES
 RUN_PARTS = 2
 RUN_PASSES = RUN_PARTS * PART_PASSES
 
+DMA_ALIGN = 256
+
 R_GATE = 0
 Z_GATE = 1
 N_GATE = 2
@@ -81,22 +83,22 @@ def tile_yarnixcellv4_pa_k_kernel(
         ones = keep.tile([P, P], BF16)
         nc.vector.memset(ones[:], 1.0)
 
-        h_sb = keep.tile([P, H], BF16)
-        angle_sb = keep.tile([P, H], BF16)
+        h_sb = keep.tile([P, H], BF16, align_bytes=DMA_ALIGN)
+        angle_sb = keep.tile([P, H], BF16, align_bytes=DMA_ALIGN)
         bias_all = keep.tile([P, N], F32)
         angle_term = keep.tile([P, H], F32)
-        h_codes = keep.tile([P, 1, P], U32, align_bytes=64)
-        h_scales = keep.tile([P, 1, P], U8, align_bytes=64)
-        hh_planes = keep.tile([P, 1, N], U8, align_bytes=64)
-        hh_tile = keep.tile([P, 1, 2 * N], U8, align_bytes=64)
+        h_codes = keep.tile([P, 1, P], U32, align_bytes=DMA_ALIGN)
+        h_scales = keep.tile([P, 1, P], U8, align_bytes=DMA_ALIGN)
+        hh_planes = keep.tile([P, 1, N], U8, align_bytes=DMA_ALIGN)
+        hh_tile = keep.tile([P, 1, 2 * N], U8, align_bytes=DMA_ALIGN)
         x_codes = []
         x_scales = []
         w_planes = []
         for part in range(PARTS):
-            x_codes.append(per_part.tile([P, PART_PASSES, P], U32, name="x_codes", align_bytes=64))
-            x_scales.append(per_part.tile([P, PART_PASSES, P], U8, name="x_scales", align_bytes=64))
+            x_codes.append(per_part.tile([P, PART_PASSES, P], U32, name="x_codes", align_bytes=DMA_ALIGN))
+            x_scales.append(per_part.tile([P, PART_PASSES, P], U8, name="x_scales", align_bytes=DMA_ALIGN))
         for run in range(IH_PASSES // RUN_PASSES):
-            w_planes.append(per_run.tile([P, RUN_PASSES, N], U8, name="w_planes", align_bytes=64))
+            w_planes.append(per_run.tile([P, RUN_PASSES, N], U8, name="w_planes", align_bytes=DMA_ALIGN))
 
         def load_scale_row(planes, scale_rows, q):
             partition = 32 * (q // 4) + q % 4
@@ -132,7 +134,7 @@ def tile_yarnixcellv4_pa_k_kernel(
 
             x_tiles = []
             for part in range(PARTS):
-                x_tile = x_pool.tile([P, PART_PASSES * K_PASS], BF16)
+                x_tile = x_pool.tile([P, PART_PASSES * K_PASS], BF16, align_bytes=DMA_ALIGN)
                 nc.sync.dma_start(
                     out=x_tile[:], in_=x[:, part * PART_PASSES * K_PASS : (part + 1) * PART_PASSES * K_PASS]
                 )
@@ -150,7 +152,7 @@ def tile_yarnixcellv4_pa_k_kernel(
                 if first_part == 0:
                     nc.sync.dma_start(out=hh_tile[:].bitcast(I32), in_=hh_words.rearrange("g p n -> p g n"))
                 for g in range(run[0] * PART_PASSES, (run[-1] + 1) * PART_PASSES, WORD_LOAD_PASSES):
-                    word_tile = weights.tile([P, WORD_LOAD_PASSES, 2 * N], U8, align_bytes=64)
+                    word_tile = weights.tile([P, WORD_LOAD_PASSES, 2 * N], U8, align_bytes=DMA_ALIGN)
                     nc.sync.dma_start(
                         out=word_tile[:].bitcast(I32),
                         in_=ih_words[g : g + WORD_LOAD_PASSES].rearrange("g p n -> p g n"),
@@ -160,7 +162,7 @@ def tile_yarnixcellv4_pa_k_kernel(
             def quantise_passes(batch_rows, codes, scales):
                 passes = codes.shape[1]
                 words = batch_rows.bitcast(F32)
-                grouped = stage.tile([P, passes, P, PACK], BF16, tag="grouped", align_bytes=64)
+                grouped = stage.tile([P, passes, P, PACK], BF16, tag="grouped", align_bytes=DMA_ALIGN)
                 grouped_words = grouped[:].bitcast(F32)
                 for j0 in range(0, passes, PASSES_PER_BANK):
                     in_bank = min(PASSES_PER_BANK, passes - j0)
@@ -240,10 +242,10 @@ def tile_yarnixcellv4_pa_k_kernel(
         r = cell.tile([P, H], F32)
         n_arg = cell.tile([P, H], F32)
         n = cell.tile([P, H], F32)
-        raw_angle = cell.tile([P, H], F32)
+        raw_angle = cell.tile([P, H], F32, align_bytes=DMA_ALIGN)
         minus_kept = cell.tile([P, H], F32)
         z_n = cell.tile([P, H], F32)
-        h_blend = cell.tile([P, H], F32)
+        h_blend = cell.tile([P, H], F32, align_bytes=DMA_ALIGN)
 
         nc.vector.tensor_tensor(out=z_gate[:], in0=sum_z[:], in1=bias_all[:, Z_GATE * H : (Z_GATE + 1) * H], op=ALU.add)
         nc.scalar.activation(out=z[:], in_=z_gate[:], func=ACT.Sigmoid)

@@ -33,6 +33,9 @@ PART_PASSES = 8
 PARTS = IH_PASSES // PART_PASSES
 WORD_LOAD_PASSES = 1
 WORD_LOADS = PART_PASSES // WORD_LOAD_PASSES
+LAST_PASSES = 8
+LAST_LOAD_PASSES = 2
+CELL_COLUMNS = H // 2
 RUN_PARTS = 2
 RUN_PASSES = RUN_PARTS * PART_PASSES
 
@@ -70,7 +73,8 @@ def tile_yarnixcellv4_pa_k_kernel(
         keep = ctx.enter_context(tc.tile_pool(name="keep", bufs=1))
         per_part = ctx.enter_context(tc.tile_pool(name="per_part", bufs=PARTS))
         per_run = ctx.enter_context(tc.tile_pool(name="per_run", bufs=PARTS // RUN_PARTS))
-        weights = ctx.enter_context(tc.tile_pool(name="weights", bufs=PARTS * WORD_LOADS))
+        weights = ctx.enter_context(tc.tile_pool(name="weights", bufs=IH_PASSES - LAST_PASSES))
+        last_weights = ctx.enter_context(tc.tile_pool(name="last_weights", bufs=LAST_PASSES // LAST_LOAD_PASSES))
         sums = ctx.enter_context(tc.psum_pool(name="sums", bufs=1))
         banks = ctx.enter_context(tc.psum_pool(name="banks", bufs=8 - GATES))
 
@@ -151,13 +155,30 @@ def tile_yarnixcellv4_pa_k_kernel(
                     load_scale_row(w_planes[first_part // RUN_PARTS][:], run_scales, q + SCALE_ROWS // 2)
                 if first_part == 0:
                     nc.sync.dma_start(out=hh_tile[:].bitcast(I32), in_=hh_words.rearrange("g p n -> p g n"))
-                for g in range(run[0] * PART_PASSES, (run[-1] + 1) * PART_PASSES, WORD_LOAD_PASSES):
+                for g in range(run[0] * PART_PASSES, min((run[-1] + 1) * PART_PASSES, IH_PASSES - LAST_PASSES)):
                     word_tile = weights.tile([P, WORD_LOAD_PASSES, 2 * N], U8, align_bytes=DMA_ALIGN)
                     nc.sync.dma_start(
                         out=word_tile[:].bitcast(I32),
                         in_=ih_words[g : g + WORD_LOAD_PASSES].rearrange("g p n -> p g n"),
                     )
                     word_tiles.append(word_tile)
+
+            last_rz = []
+            last_n = []
+            for g in range(IH_PASSES - LAST_PASSES, IH_PASSES, LAST_LOAD_PASSES):
+                rz_tile = last_weights.tile([P, LAST_LOAD_PASSES, 4 * H], U8, align_bytes=DMA_ALIGN)
+                nc.sync.dma_start(
+                    out=rz_tile[:].bitcast(I32),
+                    in_=ih_words[g : g + LAST_LOAD_PASSES, :, 0:H].rearrange("g p n -> p g n"),
+                )
+                last_rz.append((g, rz_tile))
+            for g in range(IH_PASSES - LAST_PASSES, IH_PASSES, LAST_LOAD_PASSES):
+                n_tile = last_weights.tile([P, LAST_LOAD_PASSES, 2 * H], U8, align_bytes=DMA_ALIGN)
+                nc.sync.dma_start(
+                    out=n_tile[:].bitcast(I32),
+                    in_=ih_words[g : g + LAST_LOAD_PASSES, :, H : H + H // 2].rearrange("g p n -> p g n"),
+                )
+                last_n.append((g, n_tile))
 
             def quantise_passes(batch_rows, codes, scales):
                 passes = codes.shape[1]
@@ -205,62 +226,91 @@ def tile_yarnixcellv4_pa_k_kernel(
         sum_r = sums.tile([P, H], F32)
         sum_z = sums.tile([P, H], F32)
         sum_n = sums.tile([P, H], F32)
-        gate_order = ((Z_GATE, sum_z), (R_GATE, sum_r), (N_GATE, sum_n))
+        gate_sums = {R_GATE: sum_r, Z_GATE: sum_z, N_GATE: sum_n}
 
-        def multiply(codes, scales, planes, word_tile, start, stop):
-            passes = word_tile.shape[1]
-            for gate, gate_sum in gate_order:
-                for j in range(passes):
-                    nc.tensor.matmul_mx(
-                        out=gate_sum[:],
-                        lhsT=codes[:, j, :].bitcast(FP8X4),
-                        lhsT_scale=scales[:, j, :],
-                        rhs=word_tile[:, j, gate * 2 * H : (gate + 1) * 2 * H].bitcast(FP4X4),
-                        rhs_scale=planes[:, j, gate * H : (gate + 1) * H],
-                        start=start and j == 0,
-                        stop=stop and j == passes - 1,
-                    )
-
-        multiply(h_codes, h_scales, hh_planes, hh_tile, True, False)
-        for c, word_tile in enumerate(word_tiles):
-            part = c // WORD_LOADS
-            j = (c % WORD_LOADS) * WORD_LOAD_PASSES
-            multiply(
-                x_codes[part][:, j : j + WORD_LOAD_PASSES, :],
-                x_scales[part][:, j : j + WORD_LOAD_PASSES, :],
-                w_planes[c // RUN_PASSES][:, c % RUN_PASSES : c % RUN_PASSES + WORD_LOAD_PASSES, :],
-                word_tile,
-                False,
-                c == len(word_tiles) - 1,
+        def multiply(gate, codes, scales, planes, words, start, stop):
+            nc.tensor.matmul_mx(
+                out=gate_sums[gate][:],
+                lhsT=codes.bitcast(FP8X4),
+                lhsT_scale=scales,
+                rhs=words.bitcast(FP4X4),
+                rhs_scale=planes[:, gate * H : (gate + 1) * H],
+                start=start,
+                stop=stop,
             )
 
+        def multiply_ih(gate, g, words):
+            part, j = divmod(g, PART_PASSES)
+            run, plane = divmod(g, RUN_PASSES)
+            multiply(
+                gate,
+                x_codes[part][:, j, :],
+                x_scales[part][:, j, :],
+                w_planes[run][:, plane, :],
+                words,
+                False,
+                g == IH_PASSES - 1,
+            )
+
+        for gate in (Z_GATE, R_GATE, N_GATE):
+            multiply(
+                gate, h_codes[:, 0, :], h_scales[:, 0, :], hh_planes[:, 0, :], hh_tile[:, 0, gate * 2 * H : (gate + 1) * 2 * H], True, False
+            )
+        for g, word_tile in enumerate(word_tiles):
+            for gate in (Z_GATE, R_GATE, N_GATE):
+                multiply_ih(gate, g, word_tile[:, 0, gate * 2 * H : (gate + 1) * 2 * H])
+        for first, rz_tile in last_rz:
+            for gate in (Z_GATE, R_GATE):
+                for j in range(LAST_LOAD_PASSES):
+                    multiply_ih(gate, first + j, rz_tile[:, j, gate * 2 * H : (gate + 1) * 2 * H])
+        for first, n_tile in last_n:
+            for j in range(LAST_LOAD_PASSES):
+                multiply_ih(N_GATE, first + j, n_tile[:, j, :])
+
         cell = ctx.enter_context(tc.tile_pool(name="cell", bufs=1))
+        halves = ctx.enter_context(tc.tile_pool(name="halves", bufs=H // CELL_COLUMNS))
         z_gate = cell.tile([P, H], F32)
         r_gate = cell.tile([P, H], F32)
-        n_gate = cell.tile([P, H], F32)
         z = cell.tile([P, H], F32)
         r = cell.tile([P, H], F32)
-        n_arg = cell.tile([P, H], F32)
-        n = cell.tile([P, H], F32)
         raw_angle = cell.tile([P, H], F32, align_bytes=DMA_ALIGN)
         minus_kept = cell.tile([P, H], F32)
-        z_n = cell.tile([P, H], F32)
-        h_blend = cell.tile([P, H], F32, align_bytes=DMA_ALIGN)
 
         nc.vector.tensor_tensor(out=z_gate[:], in0=sum_z[:], in1=bias_all[:, Z_GATE * H : (Z_GATE + 1) * H], op=ALU.add)
         nc.scalar.activation(out=z[:], in_=z_gate[:], func=ACT.Sigmoid)
         nc.vector.tensor_tensor(out=r_gate[:], in0=sum_r[:], in1=bias_all[:, R_GATE * H : (R_GATE + 1) * H], op=ALU.add)
         nc.scalar.activation(out=r[:], in_=r_gate[:], func=ACT.Sigmoid)
-        nc.vector.tensor_tensor(out=n_gate[:], in0=sum_n[:], in1=bias_all[:, N_GATE * H : (N_GATE + 1) * H], op=ALU.add)
-        nc.vector.tensor_tensor(out=n_arg[:], in0=r[:], in1=n_gate[:], op=ALU.mult)
-        nc.scalar.activation(out=n[:], in_=n_arg[:], func=ACT.Tanh)
+        nc.vector.scalar_tensor_tensor(
+            out=minus_kept[:], in0=z[:], scalar=1.0, in1=h_sb[:], op0=ALU.subtract, op1=ALU.mult
+        )
+        column_halves = [slice(first, first + CELL_COLUMNS) for first in range(0, H, CELL_COLUMNS)]
+        n_gates = []
+        for columns in column_halves:
+            n_gate = halves.tile([P, CELL_COLUMNS], F32)
+            nc.vector.tensor_tensor(
+                out=n_gate[:],
+                in0=sum_n[:, columns],
+                in1=bias_all[:, N_GATE * H + columns.start : N_GATE * H + columns.stop],
+                op=ALU.add,
+            )
+            n_gates.append(n_gate)
+        ns = []
+        for columns, n_gate in zip(column_halves, n_gates):
+            n_arg = halves.tile([P, CELL_COLUMNS], F32)
+            n = halves.tile([P, CELL_COLUMNS], F32)
+            nc.vector.tensor_tensor(out=n_arg[:], in0=r[:, columns], in1=n_gate[:], op=ALU.mult)
+            nc.scalar.activation(out=n[:], in_=n_arg[:], func=ACT.Tanh)
+            ns.append(n)
         nc.vector.scalar_tensor_tensor(
             out=raw_angle[:], in0=z[:], scalar=2.0 * math.pi, in1=angle_term[:], op0=ALU.mult, op1=ALU.add
         )
         nc.sync.dma_start(out=out_1, in_=raw_angle[:])
-        nc.vector.scalar_tensor_tensor(
-            out=minus_kept[:], in0=z[:], scalar=1.0, in1=h_sb[:], op0=ALU.subtract, op1=ALU.mult
-        )
-        nc.vector.tensor_tensor(out=z_n[:], in0=z[:], in1=n[:], op=ALU.mult)
-        nc.vector.tensor_tensor(out=h_blend[:], in0=z_n[:], in1=minus_kept[:], op=ALU.subtract)
-        nc.sync.dma_start(out=out_0, in_=h_blend[:])
+        z_ns = []
+        for columns, n in zip(column_halves, ns):
+            z_n = halves.tile([P, CELL_COLUMNS], F32)
+            nc.vector.tensor_tensor(out=z_n[:], in0=z[:, columns], in1=n[:], op=ALU.mult)
+            z_ns.append(z_n)
+        for columns, z_n in zip(column_halves, z_ns):
+            h_blend = halves.tile([P, CELL_COLUMNS], F32, align_bytes=DMA_ALIGN)
+            nc.vector.tensor_tensor(out=h_blend[:], in0=z_n[:], in1=minus_kept[:, columns], op=ALU.subtract)
+            nc.sync.dma_start(out=out_0[:, columns], in_=h_blend[:])

from contextlib import ExitStack

import math

import concourse.mybir as mybir
from concourse.masks import make_identity

F32 = mybir.dt.float32
BF16 = mybir.dt.bfloat16
I32 = mybir.dt.int32
U32 = mybir.dt.uint32
U8 = mybir.dt.uint8
FP8X4 = mybir.dt.float8_e4m3fn_x4
FP4X4 = mybir.dt.float4_e2m1fn_x4
ALU = mybir.AluOpType
ACT = mybir.ActivationFunctionType

P = 128
PACK = 4
K_PASS = P * PACK
I = 16384
H = 512
GATES = 3
N = GATES * H
IH_PASSES = I // K_PASS
SCALE_ROWS = K_PASS // 32

PAIRS = PACK // 2
WORDS_PER_PASS = K_PASS // 2
PASSES_PER_BANK = 2
QUANT_PASSES = 4
PART_PASSES = 8
PARTS = IH_PASSES // PART_PASSES
WORD_LOAD_PASSES = 1
WORD_LOADS = PART_PASSES // WORD_LOAD_PASSES
LAST_PASSES = 8
LAST_LOAD_PASSES = 2
CELL_COLUMNS = H // 2
RUN_PARTS = 2
RUN_PASSES = RUN_PARTS * PART_PASSES

DMA_ALIGN = 256

R_GATE = 0
Z_GATE = 1
N_GATE = 2

FLOPS = 2 * P * (I + H) * N


def tile_yarnixcellv4_pa_k_kernel(
    tc,
    x,
    h_state,
    local_angle,
    persistence,
    weight_ih_words,
    weight_ih_scales,
    weight_hh_words,
    weight_hh_scales,
    bias,
    out_0,
    out_1,
):
    nc = tc.nc
    ih_words = weight_ih_words.bitcast(I32)
    hh_words = weight_hh_words.bitcast(I32)
    ih_scales = weight_ih_scales.bitcast(I32)
    hh_scales = weight_hh_scales.bitcast(I32)

    with ExitStack() as ctx:
        ctx.enter_context(tc.manual_schedule())
        keep = ctx.enter_context(tc.tile_pool(name="keep", bufs=1))
        per_part = ctx.enter_context(tc.tile_pool(name="per_part", bufs=PARTS))
        per_run = ctx.enter_context(tc.tile_pool(name="per_run", bufs=PARTS // RUN_PARTS))
        weights = ctx.enter_context(tc.tile_pool(name="weights", bufs=IH_PASSES - LAST_PASSES))
        last_weights = ctx.enter_context(tc.tile_pool(name="last_weights", bufs=LAST_PASSES // LAST_LOAD_PASSES))
        sums = ctx.enter_context(tc.psum_pool(name="sums", bufs=1))
        banks = ctx.enter_context(tc.psum_pool(name="banks", bufs=8 - GATES))

        ident = keep.tile([P, P], F32)
        make_identity(nc, ident[:])
        warm_in = keep.tile([P, 1], F32)
        warm_out = keep.tile([P, 1], F32)
        nc.vector.memset(warm_in[:], 0.0)
        nc.scalar.activation(out=warm_out[:], in_=warm_in[:], func=ACT.Sigmoid)
        ones = keep.tile([P, P], BF16)
        nc.vector.memset(ones[:], 1.0)

        h_sb = keep.tile([P, H], BF16, align_bytes=DMA_ALIGN)
        angle_sb = keep.tile([P, H], BF16, align_bytes=DMA_ALIGN)
        bias_all = keep.tile([P, N], F32)
        angle_term = keep.tile([P, H], F32)
        h_codes = keep.tile([P, 1, P], U32, align_bytes=DMA_ALIGN)
        h_scales = keep.tile([P, 1, P], U8, align_bytes=DMA_ALIGN)
        hh_planes = keep.tile([P, 1, N], U8, align_bytes=DMA_ALIGN)
        hh_tile = keep.tile([P, 1, 2 * N], U8, align_bytes=DMA_ALIGN)
        x_codes = []
        x_scales = []
        w_planes = []
        for part in range(PARTS):
            x_codes.append(per_part.tile([P, PART_PASSES, P], U32, name="x_codes", align_bytes=DMA_ALIGN))
            x_scales.append(per_part.tile([P, PART_PASSES, P], U8, name="x_scales", align_bytes=DMA_ALIGN))
        for run in range(IH_PASSES // RUN_PASSES):
            w_planes.append(per_run.tile([P, RUN_PASSES, N], U8, name="w_planes", align_bytes=DMA_ALIGN))

        def load_scale_row(planes, scale_rows, q):
            partition = 32 * (q // 4) + q % 4
            nc.sync.dma_start(
                out=planes.bitcast(I32)[partition : partition + 1, :, :],
                in_=scale_rows[:, q : q + 1, :].rearrange("g q n -> q g n"),
            )

        def load_scale_rows(planes, scale_rows, apart):
            rows_apart = apart // 8
            for q in range(rows_apart):
                partition = 32 * (q // 4) + q % 4
                nc.sync.dma_start(
                    out=planes.bitcast(I32)[partition:P:apart, :, :],
                    in_=scale_rows[:, q:SCALE_ROWS:rows_apart, :].rearrange("g q n -> q g n"),
                )

        with ExitStack() as early:
            x_pool = early.enter_context(tc.tile_pool(name="x_pool", bufs=PARTS))
            stage = early.enter_context(tc.tile_pool(name="stage", bufs=3))
            rows = early.enter_context(tc.tile_pool(name="rows", bufs=1))

            row = rows.tile([P, N + H], BF16)
            nc.vector.memset(row[:].bitcast(I32), 0)
            nc.vector.memset(hh_planes[:].bitcast(I32), 0)
            for planes in w_planes:
                nc.vector.memset(planes[:].bitcast(I32), 0)

            nc.gpsimd.dma_start(out=h_sb[:], in_=h_state)
            nc.gpsimd.dma_start(out=row[0:1, 0:N], in_=bias.unsqueeze(0))
            nc.gpsimd.dma_start(out=row[0:1, N : N + H], in_=persistence.unsqueeze(0))
            nc.gpsimd.dma_start(out=angle_sb[:], in_=local_angle)

            x_tiles = []
            for part in range(PARTS):
                x_tile = x_pool.tile([P, PART_PASSES * K_PASS], BF16, align_bytes=DMA_ALIGN)
                nc.sync.dma_start(
                    out=x_tile[:], in_=x[:, part * PART_PASSES * K_PASS : (part + 1) * PART_PASSES * K_PASS]
                )
                x_tiles.append(x_tile)
                if part == PARTS // 2 - 1:
                    load_scale_rows(hh_planes[:], hh_scales, 32)

            word_tiles = []
            for first_part in range(0, PARTS, RUN_PARTS):
                run = range(first_part, first_part + RUN_PARTS)
                run_scales = ih_scales[run[0] * PART_PASSES : run[0] * PART_PASSES + RUN_PASSES]
                for q in range(SCALE_ROWS // 2):
                    load_scale_row(w_planes[first_part // RUN_PARTS][:], run_scales, q)
                    load_scale_row(w_planes[first_part // RUN_PARTS][:], run_scales, q + SCALE_ROWS // 2)
                if first_part == 0:
                    nc.sync.dma_start(out=hh_tile[:].bitcast(I32), in_=hh_words.rearrange("g p n -> p g n"))
                for g in range(run[0] * PART_PASSES, min((run[-1] + 1) * PART_PASSES, IH_PASSES - LAST_PASSES)):
                    word_tile = weights.tile([P, WORD_LOAD_PASSES, 2 * N], U8, align_bytes=DMA_ALIGN)
                    nc.sync.dma_start(
                        out=word_tile[:].bitcast(I32),
                        in_=ih_words[g : g + WORD_LOAD_PASSES].rearrange("g p n -> p g n"),
                    )
                    word_tiles.append(word_tile)

            last_rz = []
            last_n = []
            for g in range(IH_PASSES - LAST_PASSES, IH_PASSES, LAST_LOAD_PASSES):
                rz_tile = last_weights.tile([P, LAST_LOAD_PASSES, 4 * H], U8, align_bytes=DMA_ALIGN)
                nc.sync.dma_start(
                    out=rz_tile[:].bitcast(I32),
                    in_=ih_words[g : g + LAST_LOAD_PASSES, :, 0:H].rearrange("g p n -> p g n"),
                )
                last_rz.append((g, rz_tile))
            for g in range(IH_PASSES - LAST_PASSES, IH_PASSES, LAST_LOAD_PASSES):
                n_tile = last_weights.tile([P, LAST_LOAD_PASSES, 2 * H], U8, align_bytes=DMA_ALIGN)
                nc.sync.dma_start(
                    out=n_tile[:].bitcast(I32),
                    in_=ih_words[g : g + LAST_LOAD_PASSES, :, H : H + H // 2].rearrange("g p n -> p g n"),
                )
                last_n.append((g, n_tile))

            def quantise_passes(batch_rows, codes, scales):
                passes = codes.shape[1]
                words = batch_rows.bitcast(F32)
                grouped = stage.tile([P, passes, P, PACK], BF16, tag="grouped", align_bytes=DMA_ALIGN)
                grouped_words = grouped[:].bitcast(F32)
                for j0 in range(0, passes, PASSES_PER_BANK):
                    in_bank = min(PASSES_PER_BANK, passes - j0)
                    bank = banks.tile([P, in_bank, PAIRS, P], F32, tag="bank")
                    for j in range(in_bank):
                        first_word = (j0 + j) * WORDS_PER_PASS
                        for u in range(PAIRS):
                            nc.tensor.transpose(
                                bank[:, j, u, :],
                                words[:, first_word + u : first_word + WORDS_PER_PASS : PAIRS],
                                ident[:],
                            )
                    nc.scalar.copy(
                        out=grouped_words[:, j0 : j0 + in_bank, :, :],
                        in_=bank[:].rearrange("p j u b -> p j b u"),
                    )
                nc.vector.quantize_mx(
                    out=codes.rearrange("p g b -> p (g b)").bitcast(FP8X4),
                    scales=scales.rearrange("p g b -> p (g b)"),
                    in_=grouped[:].rearrange("p g b t -> p (g b t)"),
                )

            for part in range(PARTS):
                for j in range(0, PART_PASSES, QUANT_PASSES):
                    quantise_passes(
                        x_tiles[part][:, j * K_PASS : (j + QUANT_PASSES) * K_PASS],
                        x_codes[part][:, j : j + QUANT_PASSES, :],
                        x_scales[part][:, j : j + QUANT_PASSES, :],
                    )
            quantise_passes(h_sb[:], h_codes[:], h_scales[:])

            for c in range(GATES + 1):
                spread = banks.tile([P, H], F32, tag="bank")
                nc.tensor.matmul(out=spread[:], lhsT=ones[:], rhs=row[:, c * H : (c + 1) * H], start=True, stop=True)
                if c < GATES:
                    nc.scalar.copy(out=bias_all[:, c * H : (c + 1) * H], in_=spread[:])
                else:
                    nc.vector.tensor_tensor(out=angle_term[:], in0=spread[:], in1=angle_sb[:], op=ALU.mult)

        sum_r = sums.tile([P, H], F32)
        sum_z = sums.tile([P, H], F32)
        sum_n = sums.tile([P, H], F32)
        gate_sums = {R_GATE: sum_r, Z_GATE: sum_z, N_GATE: sum_n}

        def multiply(gate, codes, scales, planes, words, start, stop):
            nc.tensor.matmul_mx(
                out=gate_sums[gate][:],
                lhsT=codes.bitcast(FP8X4),
                lhsT_scale=scales,
                rhs=words.bitcast(FP4X4),
                rhs_scale=planes[:, gate * H : (gate + 1) * H],
                start=start,
                stop=stop,
            )

        def multiply_ih(gate, g, words):
            part, j = divmod(g, PART_PASSES)
            run, plane = divmod(g, RUN_PASSES)
            multiply(
                gate,
                x_codes[part][:, j, :],
                x_scales[part][:, j, :],
                w_planes[run][:, plane, :],
                words,
                False,
                g == IH_PASSES - 1,
            )

        for gate in (Z_GATE, R_GATE, N_GATE):
            multiply(
                gate, h_codes[:, 0, :], h_scales[:, 0, :], hh_planes[:, 0, :], hh_tile[:, 0, gate * 2 * H : (gate + 1) * 2 * H], True, False
            )
        for g, word_tile in enumerate(word_tiles):
            for gate in (Z_GATE, R_GATE, N_GATE):
                multiply_ih(gate, g, word_tile[:, 0, gate * 2 * H : (gate + 1) * 2 * H])
        for first, rz_tile in last_rz:
            for gate in (Z_GATE, R_GATE):
                for j in range(LAST_LOAD_PASSES):
                    multiply_ih(gate, first + j, rz_tile[:, j, gate * 2 * H : (gate + 1) * 2 * H])
        for first, n_tile in last_n:
            for j in range(LAST_LOAD_PASSES):
                multiply_ih(N_GATE, first + j, n_tile[:, j, :])

        cell = ctx.enter_context(tc.tile_pool(name="cell", bufs=1))
        halves = ctx.enter_context(tc.tile_pool(name="halves", bufs=H // CELL_COLUMNS))
        z_gate = cell.tile([P, H], F32)
        r_gate = cell.tile([P, H], F32)
        z = cell.tile([P, H], F32)
        r = cell.tile([P, H], F32)
        raw_angle = cell.tile([P, H], F32, align_bytes=DMA_ALIGN)
        minus_kept = cell.tile([P, H], F32)

        nc.vector.tensor_tensor(out=z_gate[:], in0=sum_z[:], in1=bias_all[:, Z_GATE * H : (Z_GATE + 1) * H], op=ALU.add)
        nc.scalar.activation(out=z[:], in_=z_gate[:], func=ACT.Sigmoid)
        nc.vector.tensor_tensor(out=r_gate[:], in0=sum_r[:], in1=bias_all[:, R_GATE * H : (R_GATE + 1) * H], op=ALU.add)
        nc.scalar.activation(out=r[:], in_=r_gate[:], func=ACT.Sigmoid)
        nc.vector.scalar_tensor_tensor(
            out=minus_kept[:], in0=z[:], scalar=1.0, in1=h_sb[:], op0=ALU.subtract, op1=ALU.mult
        )
        column_halves = [slice(first, first + CELL_COLUMNS) for first in range(0, H, CELL_COLUMNS)]
        n_gates = []
        for columns in column_halves:
            n_gate = halves.tile([P, CELL_COLUMNS], F32)
            nc.vector.tensor_tensor(
                out=n_gate[:],
                in0=sum_n[:, columns],
                in1=bias_all[:, N_GATE * H + columns.start : N_GATE * H + columns.stop],
                op=ALU.add,
            )
            n_gates.append(n_gate)
        ns = []
        for columns, n_gate in zip(column_halves, n_gates):
            n_arg = halves.tile([P, CELL_COLUMNS], F32)
            n = halves.tile([P, CELL_COLUMNS], F32)
            nc.vector.tensor_tensor(out=n_arg[:], in0=r[:, columns], in1=n_gate[:], op=ALU.mult)
            nc.scalar.activation(out=n[:], in_=n_arg[:], func=ACT.Tanh)
            ns.append(n)
        nc.vector.scalar_tensor_tensor(
            out=raw_angle[:], in0=z[:], scalar=2.0 * math.pi, in1=angle_term[:], op0=ALU.mult, op1=ALU.add
        )
        nc.sync.dma_start(out=out_1, in_=raw_angle[:])
        z_ns = []
        for columns, n in zip(column_halves, ns):
            z_n = halves.tile([P, CELL_COLUMNS], F32)
            nc.vector.tensor_tensor(out=z_n[:], in0=z[:, columns], in1=n[:], op=ALU.mult)
            z_ns.append(z_n)
        for columns, z_n in zip(column_halves, z_ns):
            h_blend = halves.tile([P, CELL_COLUMNS], F32, align_bytes=DMA_ALIGN)
            nc.vector.tensor_tensor(out=h_blend[:], in0=z_n[:], in1=minus_kept[:, columns], op=ALU.subtract)
            nc.sync.dma_start(out=out_0[:, columns], in_=h_blend[:])
